import numpy as np
import ml_dtypes


def mxq(x, axis, fmt="e4m3"):
    dtype, down = {"e4m3": (ml_dtypes.float8_e4m3fn, 7), "e5m2": (ml_dtypes.float8_e5m2, 14)}[fmt]
    v = np.moveaxis(np.asarray(x, np.float32).astype(ml_dtypes.bfloat16).astype(np.float64), axis, -1)
    blocks = v.reshape(v.shape[:-1] + (-1, 32))
    amax = np.abs(blocks).max(-1, keepdims=True)
    byte = np.maximum(np.where(amax > 0, np.frexp(amax)[1] - 1 + 127, 0) - down, 1)
    scale = np.exp2(byte - 127.0)
    codes = (blocks / scale).astype(np.float32).astype(dtype).astype(np.float64)
    return np.moveaxis((codes * scale).reshape(v.shape), -1, axis)


WIDE = False


def mx_kscale(k):
    if not WIDE:
        return np.ones(k)
    levels = np.array([10, -10, 5, -5, 0])
    a = np.random.permutation(np.resize(levels, k // 512 * 4)).reshape(k // 512, 4)
    idx = np.arange(k)
    return np.exp2(a[idx // 512, idx % 128 // 32])


BF16 = ml_dtypes.bfloat16


def bf(x):
    return np.asarray(x, np.float32).astype(BF16)


def f64(x):
    return np.asarray(x).astype(np.float64)


B, S, D, H, DK, F = 4, 2048, 512, 2, 128, 4096
E = H * DK
EPS = 1e-5


def rmsnorm(a, g):
    rms = np.sqrt(np.sum(a * a, axis=-1, keepdims=True) / a.shape[-1] + EPS)
    return a / rms * g


def heads(y):
    return y.reshape(B, S, H, DK).transpose(0, 2, 1, 3)


def setup_inputs():
    s = mx_kscale(D)
    quiet = np.where(np.random.random((B, S, 1)) < 0.1, 0.003, 1.0)
    return {"x": bf(np.random.standard_normal((B, S, D)) * quiet),
            "g1": bf((1.0 + 0.1 * np.random.standard_normal(D)) * s),
            "wq": bf(np.random.standard_normal((E, D)) / np.sqrt(D) / s),
            "wk": bf(np.random.standard_normal((E, D)) / np.sqrt(D) / s),
            "wv": bf(np.random.standard_normal((E, D)) * 2.0 / np.sqrt(D) / s)}


def reference(x, g1, wq, wk, wv):
    xq = mxq(rmsnorm(f64(x), f64(g1)), 2, "e4m3")
    q = heads(xq @ mxq(f64(wq), 1, "e4m3").T)
    k = heads(xq @ mxq(f64(wk), 1, "e4m3").T)
    v = heads(xq @ mxq(f64(wv), 1, "e4m3").T)
    return q, k, v

@@ -1,0 +1,200 @@
+from contextlib import ExitStack
+
+import concourse.mybir as mybir
+from concourse.masks import make_identity
+
+F32 = mybir.dt.float32
+BF16 = mybir.dt.bfloat16
+U32 = mybir.dt.uint32
+U8 = mybir.dt.uint8
+FP8X4 = mybir.dt.float8_e4m3fn_x4
+ACT = mybir.ActivationFunctionType
+ALU = mybir.AluOpType
+
+P = 128
+B = 4
+S = 2048
+D = 512
+E = 256
+EPS = 1e-5
+PACK = 4
+JB = S // P
+CH = 4
+NT = B * JB
+NOUT = 3 * E
+STAT_GROUPS = [2, 2] + [4] * 15
+PIECES = [4] * 15 + [2, 2]
+
+FLOPS = 2 * B * S * D * NOUT
+
+
+def tile_transformerblock_pa_t_kernel(tc, x, g1, wq, wk, wv, out_0, out_1, out_2):
+    nc = tc.nc
+    outs = [out_0, out_1, out_2]
+    ws = [wq, wk, wv]
+    with ExitStack() as ctx:
+        const = ctx.enter_context(tc.tile_pool(name="const", bufs=1))
+        xpool = ctx.enter_context(tc.tile_pool(name="xpool", bufs=1))
+        stat = ctx.enter_context(tc.tile_pool(name="stat", bufs=1))
+        work = ctx.enter_context(tc.tile_pool(name="work", bufs=3))
+        opool = ctx.enter_context(tc.tile_pool(name="opool", bufs=6))
+        pt = ctx.enter_context(tc.psum_pool(name="pt", bufs=4))
+        po = ctx.enter_context(tc.psum_pool(name="po", bufs=4))
+
+        n_chunks = NT // CH
+        xs = []
+        for c in range(n_chunks):
+            xs.append(xpool.tile([P, CH, D], BF16, name="x%d" % c))
+
+        def load_x(c):
+            b, j0 = divmod(c * CH, JB)
+            xv = x[b].rearrange("(p j) d -> p j d", j=JB)
+            nc.sync.dma_start(out=xs[c][:], in_=xv[:, j0 : j0 + CH, :])
+
+        load_x(0)
+        g_rows = const.tile([P, P], BF16)
+        nc.vector.memset(g_rows[:], 0.0)
+        nc.sync.dma_start(out=g_rows[0:PACK, :], in_=g1.rearrange("(t p) -> t p", p=P))
+        w_raw = []
+        for i in range(3):
+            wr = const.tile([P, 2, D], BF16, name="w_raw%d" % i)
+            nc.sync.dma_start(out=wr[:], in_=ws[i].rearrange("(a p) k -> p a k", p=P))
+            w_raw.append(wr)
+        for c in range(1, n_chunks):
+            load_x(c)
+
+        ident_f = const.tile([P, P], F32)
+        make_identity(nc, ident_f[:])
+        ident_b = const.tile([P, P], BF16)
+        make_identity(nc, ident_b[:])
+        one_t = const.tile([P, 1], F32)
+        nc.vector.memset(one_t[:], 1.0)
+        warm = const.tile([P, 1], F32)
+        nc.scalar.activation(out=warm[:], in_=one_t[:], func=ACT.Sqrt)
+
+        g_ps = pt.tile([P, P], BF16, tag="t")
+        nc.tensor.transpose(out=g_ps[:], in_=g_rows[:], identity=ident_b[:])
+        gain = const.tile([P, PACK], F32)
+        nc.vector.tensor_copy(out=gain[:], in_=g_ps[:, 0:PACK])
+
+        w_grp = const.tile([P, NOUT, PACK], BF16, align_bytes=64)
+        w_codes = const.tile([P, NOUT], U32, align_bytes=64)
+        w_scales = const.tile([P, NOUT], U8, align_bytes=64)
+        for i in range(3):
+            for a in range(2):
+                w_ps = pt.tile([P, PACK, P], BF16, tag="t")
+                for t in range(PACK):
+                    nc.tensor.transpose(
+                        out=w_ps[:, t, :], in_=w_raw[i][:, a, t * P : (t + 1) * P], identity=ident_b[:]
+                    )
+                n0 = i * E + a * P
+                nc.vector.tensor_copy(
+                    out=w_grp[:, n0 : n0 + P, :], in_=w_ps[:].rearrange("p t n -> p n t")
+                )
+        for i in range(3):
+            nc.vector.quantize_mx(
+                out=w_codes[:, i * E : (i + 1) * E].bitcast(FP8X4),
+                scales=w_scales[:, i * E : (i + 1) * E],
+                in_=w_grp[:, i * E : (i + 1) * E, :].rearrange("p n t -> p (n t)"),
+            )
+
+        gain_b = gain[:].unsqueeze(1).to_broadcast([P, P, PACK])
+
+        piece_of = []
+        k0 = 0
+        for n in PIECES:
+            for q in range(n):
+                piece_of.append((k0, n))
+            k0 += n
+
+        def x_tile(k):
+            return xs[k // CH][:, k % CH, :]
+
+        o_sb = None
+        first = 0
+        for gi, gn in enumerate(STAT_GROUPS):
+            ss = stat.tile([P, gn], F32, name="ss%d" % gi)
+            var = stat.tile([P, gn], F32, name="var%d" % gi)
+            inv = stat.tile([P, gn], F32, name="inv%d" % gi)
+            rstd = stat.tile([P, gn], F32, name="rstd%d" % gi)
+            for q in range(gn):
+                junk = work.tile([P, D], BF16, tag="junk")
+                nc.scalar.activation(
+                    out=junk[:], in_=x_tile(first + q), func=ACT.Square, accum_out=ss[:, q : q + 1]
+                )
+            nc.vector.tensor_scalar(
+                out=var[:], in0=ss[:], scalar1=1.0 / D, scalar2=EPS, op0=ALU.mult, op1=ALU.add
+            )
+            nc.vector.reciprocal(out=inv[:], in_=var[:])
+            nc.scalar.activation(out=rstd[:], in_=inv[:], func=ACT.Sqrt)
+            for half in range(gn // 2):
+                tile0 = first + half * 2
+                pair = tile0 // 2
+                pk0, pn = piece_of[tile0]
+                js = tile0 - pk0
+                if js == 0:
+                    o_sb = opool.tile([P, 6, pn, P], F32, tag="o_sb")
+                grp = work.tile([P, 2, P, PACK], BF16, tag="grp", align_bytes=64)
+                codes = work.tile([P, 2 * P], U32, tag="codes", align_bytes=64)
+                scl = work.tile([P, 2 * P], U8, tag="scl", align_bytes=64)
+                for a in range(2):
+                    q = half * 2 + a
+                    y = work.tile([P, D], F32, tag="y", bufs=6)
+                    nc.gpsimd.tensor_scalar(
+                        out=y[:], in0=x_tile(tile0 + a), scalar1=rstd[:, q : q + 1], scalar2=1.0,
+                        op0=ALU.mult, op1=ALU.mult,
+                    )
+                    y_ps = pt.tile([P, PACK, P], F32, tag="t")
+                    for t in range(PACK):
+                        nc.tensor.transpose(
+                            out=y_ps[:, t, :], in_=y[:, t * P : (t + 1) * P], identity=ident_f[:]
+                        )
+                    nc.vector.tensor_tensor(
+                        out=grp[:, a, :, :], in0=y_ps[:].rearrange("p t r -> p r t"), in1=gain_b,
+                        op=ALU.mult,
+                    )
+                nc.vector.quantize_mx(
+                    out=codes[:].bitcast(FP8X4), scales=scl[:],
+                    in_=grp[:].rearrange("p a r t -> p (a r t)"),
+                )
+                banks = []
+                for a in range(2):
+                    o_qk = po.tile([P, 2 * E], F32, tag="o")
+                    nc.tensor.matmul_mx(
+                        out=o_qk[:],
+                        lhsT=codes[:, a * P : (a + 1) * P].bitcast(FP8X4),
+                        lhsT_scale=scl[:, a * P : (a + 1) * P],
+                        rhs=w_codes[:, 0 : 2 * E].bitcast(FP8X4),
+                        rhs_scale=w_scales[:, 0 : 2 * E],
+                        start=True, stop=True,
+                    )
+                    banks.append(o_qk)
+                o_v = po.tile([P, 2 * E], F32, tag="o")
+                for a in range(2):
+                    nc.tensor.matmul_mx(
+                        out=o_v[:, a * E : (a + 1) * E],
+                        lhsT=codes[:, a * P : (a + 1) * P].bitcast(FP8X4),
+                        lhsT_scale=scl[:, a * P : (a + 1) * P],
+                        rhs=w_codes[:, 2 * E : 3 * E].bitcast(FP8X4),
+                        rhs_scale=w_scales[:, 2 * E : 3 * E],
+                        start=True, stop=True,
+                    )
+                for a in range(2):
+                    dst = o_sb[:, 0:4, js + a, :]
+                    src = banks[a][:].rearrange("p (g d) -> p g d", d=P)
+                    if a == 1 and pair % 3 == 2:
+                        nc.vector.tensor_copy(out=dst, in_=src)
+                    else:
+                        nc.scalar.copy(out=dst, in_=src)
+                nc.vector.tensor_copy(
+                    out=o_sb[:, 4:6, js : js + 2, :].rearrange("p g a d -> p a g d"),
+                    in_=o_v[:].rearrange("p (a g d) -> p a g d", a=2, d=P),
+                )
+                if js + 2 == pn:
+                    b, j0 = divmod(pk0, JB)
+                    for i in range(3):
+                        ov = outs[i][b].rearrange("h (p j) d -> p h j d", j=JB)
+                        nc.sync.dma_start(
+                            out=ov[:, :, j0 : j0 + pn, :], in_=o_sb[:, 2 * i : 2 * i + 2, :, :]
+                        )
+            first += gn

@@ -21,9 +21,14 @@ PACK = 4
 JB = S // P
 CH = 4
 NT = B * JB
+NP = NT // 2
 NOUT = 3 * E
 STAT_GROUPS = [2, 2] + [4] * 15
 PIECES = [4] * 15 + [2, 2]
+HEAD_STATS = 12
+LEAD = 3
+S_BANKS = [1, 2]
+S_ALL_FROM = 26
 
 FLOPS = 2 * B * S * D * NOUT
 
@@ -40,6 +45,7 @@ def tile_transformerblock_pa_t_kernel(tc, x, g1, wq, wk, wv, out_0, out_1, out_2
         opool = ctx.enter_context(tc.tile_pool(name="opool", bufs=6))
         pt = ctx.enter_context(tc.psum_pool(name="pt", bufs=4))
         po = ctx.enter_context(tc.psum_pool(name="po", bufs=4))
+        ctx.enter_context(tc.manual_schedule())
 
         n_chunks = NT // CH
         xs = []
@@ -50,6 +56,9 @@ def tile_transformerblock_pa_t_kernel(tc, x, g1, wq, wk, wv, out_0, out_1, out_2
             b, j0 = divmod(c * CH, JB)
             xv = x[b].rearrange("(p j) d -> p j d", j=JB)
             nc.sync.dma_start(out=xs[c][:], in_=xv[:, j0 : j0 + CH, :])
+
+        def x_tile(k):
+            return xs[k // CH][:, k % CH, :]
 
         load_x(0)
         g_rows = const.tile([P, P], BF16)
@@ -63,138 +72,230 @@ def tile_transformerblock_pa_t_kernel(tc, x, g1, wq, wk, wv, out_0, out_1, out_2
         for c in range(1, n_chunks):
             load_x(c)
 
-        ident_f = const.tile([P, P], F32)
-        make_identity(nc, ident_f[:])
         ident_b = const.tile([P, P], BF16)
         make_identity(nc, ident_b[:])
+        ident_f = const.tile([P, P], F32)
+        make_identity(nc, ident_f[:])
         one_t = const.tile([P, 1], F32)
         nc.vector.memset(one_t[:], 1.0)
         warm = const.tile([P, 1], F32)
         nc.scalar.activation(out=warm[:], in_=one_t[:], func=ACT.Sqrt)
 
-        g_ps = pt.tile([P, P], BF16, tag="t")
-        nc.tensor.transpose(out=g_ps[:], in_=g_rows[:], identity=ident_b[:])
         gain = const.tile([P, PACK], F32)
-        nc.vector.tensor_copy(out=gain[:], in_=g_ps[:, 0:PACK])
-
+        gain_b = gain[:].unsqueeze(1).to_broadcast([P, P, PACK])
         w_grp = const.tile([P, NOUT, PACK], BF16, align_bytes=64)
         w_codes = const.tile([P, NOUT], U32, align_bytes=64)
         w_scales = const.tile([P, NOUT], U8, align_bytes=64)
-        for i in range(3):
-            for a in range(2):
-                w_ps = pt.tile([P, PACK, P], BF16, tag="t")
-                for t in range(PACK):
-                    nc.tensor.transpose(
-                        out=w_ps[:, t, :], in_=w_raw[i][:, a, t * P : (t + 1) * P], identity=ident_b[:]
-                    )
-                n0 = i * E + a * P
-                nc.vector.tensor_copy(
-                    out=w_grp[:, n0 : n0 + P, :], in_=w_ps[:].rearrange("p t n -> p n t")
+
+        def gain_columns():
+            g_ps = pt.tile([P, P], BF16, tag="t")
+            nc.tensor.transpose(out=g_ps[:], in_=g_rows[:], identity=ident_b[:])
+            nc.vector.tensor_copy(out=gain[:], in_=g_ps[:, 0:PACK])
+
+        w_ps = {}
+
+        def w_transposes(u):
+            w_ps[u] = pt.tile([P, PACK, P], BF16, tag="t", name="w_ps%d" % u)
+            for t in range(PACK):
+                nc.tensor.transpose(
+                    out=w_ps[u][:, t, :], in_=w_raw[u // 2][:, u % 2, t * P : (t + 1) * P],
+                    identity=ident_b[:],
                 )
-        for i in range(3):
+
+        def w_regroup(u):
+            nc.vector.tensor_copy(
+                out=w_grp[:, u * P : (u + 1) * P, :], in_=w_ps[u][:].rearrange("p t n -> p n t")
+            )
+
+        def w_quantise(i):
             nc.vector.quantize_mx(
                 out=w_codes[:, i * E : (i + 1) * E].bitcast(FP8X4),
                 scales=w_scales[:, i * E : (i + 1) * E],
                 in_=w_grp[:, i * E : (i + 1) * E, :].rearrange("p n t -> p (n t)"),
             )
 
-        gain_b = gain[:].unsqueeze(1).to_broadcast([P, P, PACK])
-
+        group_of = []
+        k0 = 0
+        for gi, gn in enumerate(STAT_GROUPS):
+            for q in range(gn):
+                group_of.append((gi, k0, gn))
+            k0 += gn
         piece_of = []
         k0 = 0
-        for n in PIECES:
-            for q in range(n):
-                piece_of.append((k0, n))
-            k0 += n
+        for pn in PIECES:
+            for q in range(pn):
+                piece_of.append((k0, pn))
+            k0 += pn
 
-        def x_tile(k):
-            return xs[k // CH][:, k % CH, :]
+        ss = {}
+        rms = {}
+        rstd = {}
+        y = {}
+        y_ps = {}
+        grp = {}
+        codes = {}
+        scl = {}
+        banks = {}
+        o_sb = {}
+        progress = {"stats": 0}
 
-        o_sb = None
-        first = 0
-        for gi, gn in enumerate(STAT_GROUPS):
-            ss = stat.tile([P, gn], F32, name="ss%d" % gi)
-            var = stat.tile([P, gn], F32, name="var%d" % gi)
-            inv = stat.tile([P, gn], F32, name="inv%d" % gi)
-            rstd = stat.tile([P, gn], F32, name="rstd%d" % gi)
-            for q in range(gn):
+        def statistics(count):
+            for q in range(count):
+                k = progress["stats"]
+                if k >= NT:
+                    return
+                gi, g0, gn = group_of[k]
+                if k == g0:
+                    ss[gi] = stat.tile([P, gn], F32, name="ss%d" % gi)
                 junk = work.tile([P, D], BF16, tag="junk")
                 nc.scalar.activation(
-                    out=junk[:], in_=x_tile(first + q), func=ACT.Square, accum_out=ss[:, q : q + 1]
+                    out=junk[:], in_=x_tile(k), func=ACT.Square, accum_out=ss[gi][:, k - g0 : k - g0 + 1]
                 )
-            nc.vector.tensor_scalar(
-                out=var[:], in0=ss[:], scalar1=1.0 / D, scalar2=EPS, op0=ALU.mult, op1=ALU.add
+                if k == g0 + gn - 1:
+                    var = stat.tile([P, gn], F32, name="var%d" % gi)
+                    rms[gi] = stat.tile([P, gn], F32, name="rms%d" % gi)
+                    nc.scalar.activation(out=var[:], in_=ss[gi][:], func=ACT.Copy, bias=EPS, scale=1.0 / D)
+                    nc.scalar.activation(out=rms[gi][:], in_=var[:], func=ACT.Sqrt)
+                progress["stats"] = k + 1
+
+        def release(j):
+            if j >= NP:
+                return
+            gi, g0, gn = group_of[2 * j]
+            rstd[j] = stat.tile([P, 2], F32, name="rstd%d" % j)
+            nc.vector.reciprocal(out=rstd[j][:], in_=rms[gi][:, 2 * j - g0 : 2 * j - g0 + 2])
+            for a in range(2):
+                k = 2 * j + a
+                y[k] = work.tile([P, D], F32, tag="y", bufs=6, name="y%d" % k)
+                nc.gpsimd.tensor_scalar(
+                    out=y[k][:], in0=x_tile(k), scalar1=rstd[j][:, a : a + 1], scalar2=1.0,
+                    op0=ALU.mult, op1=ALU.mult,
+                )
+
+        def transposes(k):
+            y_ps[k] = pt.tile([P, PACK, P], F32, tag="t", name="y_ps%d" % k)
+            for t in range(PACK):
+                nc.tensor.transpose(
+                    out=y_ps[k][:, t, :], in_=y[k][:, t * P : (t + 1) * P], identity=ident_f[:]
+                )
+
+        def norm(k):
+            j = k // 2
+            if k % 2 == 0:
+                grp[j] = work.tile([P, 2, P, PACK], BF16, tag="grp", align_bytes=64, name="grp%d" % j)
+            nc.vector.tensor_tensor(
+                out=grp[j][:, k % 2, :, :], in0=y_ps[k][:].rearrange("p t r -> p r t"), in1=gain_b,
+                op=ALU.mult,
             )
-            nc.vector.reciprocal(out=inv[:], in_=var[:])
-            nc.scalar.activation(out=rstd[:], in_=inv[:], func=ACT.Sqrt)
-            for half in range(gn // 2):
-                tile0 = first + half * 2
-                pair = tile0 // 2
-                pk0, pn = piece_of[tile0]
-                js = tile0 - pk0
-                if js == 0:
-                    o_sb = opool.tile([P, 6, pn, P], F32, tag="o_sb")
-                grp = work.tile([P, 2, P, PACK], BF16, tag="grp", align_bytes=64)
-                codes = work.tile([P, 2 * P], U32, tag="codes", align_bytes=64)
-                scl = work.tile([P, 2 * P], U8, tag="scl", align_bytes=64)
-                for a in range(2):
-                    q = half * 2 + a
-                    y = work.tile([P, D], F32, tag="y", bufs=6)
-                    nc.gpsimd.tensor_scalar(
-                        out=y[:], in0=x_tile(tile0 + a), scalar1=rstd[:, q : q + 1], scalar2=1.0,
-                        op0=ALU.mult, op1=ALU.mult,
-                    )
-                    y_ps = pt.tile([P, PACK, P], F32, tag="t")
-                    for t in range(PACK):
-                        nc.tensor.transpose(
-                            out=y_ps[:, t, :], in_=y[:, t * P : (t + 1) * P], identity=ident_f[:]
-                        )
-                    nc.vector.tensor_tensor(
-                        out=grp[:, a, :, :], in0=y_ps[:].rearrange("p t r -> p r t"), in1=gain_b,
-                        op=ALU.mult,
-                    )
-                nc.vector.quantize_mx(
-                    out=codes[:].bitcast(FP8X4), scales=scl[:],
-                    in_=grp[:].rearrange("p a r t -> p (a r t)"),
+
+        def quantise(j):
+            codes[j] = work.tile([P, 2 * P], U32, tag="codes", align_bytes=64, name="codes%d" % j)
+            scl[j] = work.tile([P, 2 * P], U8, tag="scl", align_bytes=64, name="scl%d" % j)
+            nc.vector.quantize_mx(
+                out=codes[j][:].bitcast(FP8X4), scales=scl[j][:],
+                in_=grp[j][:].rearrange("p a r t -> p (a r t)"),
+            )
+
+        def project(j):
+            for a in range(2):
+                banks[(j, a)] = po.tile([P, 2 * E], F32, tag="o", name="o%d_%d" % (j, a))
+                nc.tensor.matmul_mx(
+                    out=banks[(j, a)][:],
+                    lhsT=codes[j][:, a * P : (a + 1) * P].bitcast(FP8X4),
+                    lhsT_scale=scl[j][:, a * P : (a + 1) * P],
+                    rhs=w_codes[:, 0 : 2 * E].bitcast(FP8X4),
+                    rhs_scale=w_scales[:, 0 : 2 * E],
+                    start=True, stop=True,
                 )
-                banks = []
-                for a in range(2):
-                    o_qk = po.tile([P, 2 * E], F32, tag="o")
-                    nc.tensor.matmul_mx(
-                        out=o_qk[:],
-                        lhsT=codes[:, a * P : (a + 1) * P].bitcast(FP8X4),
-                        lhsT_scale=scl[:, a * P : (a + 1) * P],
-                        rhs=w_codes[:, 0 : 2 * E].bitcast(FP8X4),
-                        rhs_scale=w_scales[:, 0 : 2 * E],
-                        start=True, stop=True,
-                    )
-                    banks.append(o_qk)
-                o_v = po.tile([P, 2 * E], F32, tag="o")
-                for a in range(2):
-                    nc.tensor.matmul_mx(
-                        out=o_v[:, a * E : (a + 1) * E],
-                        lhsT=codes[:, a * P : (a + 1) * P].bitcast(FP8X4),
-                        lhsT_scale=scl[:, a * P : (a + 1) * P],
-                        rhs=w_codes[:, 2 * E : 3 * E].bitcast(FP8X4),
-                        rhs_scale=w_scales[:, 2 * E : 3 * E],
-                        start=True, stop=True,
-                    )
-                for a in range(2):
-                    dst = o_sb[:, 0:4, js + a, :]
-                    src = banks[a][:].rearrange("p (g d) -> p g d", d=P)
-                    if a == 1 and pair % 3 == 2:
-                        nc.vector.tensor_copy(out=dst, in_=src)
+            banks[(j, 2)] = po.tile([P, 2 * E], F32, tag="o", name="o%d_2" % j)
+            for a in range(2):
+                nc.tensor.matmul_mx(
+                    out=banks[(j, 2)][:, a * E : (a + 1) * E],
+                    lhsT=codes[j][:, a * P : (a + 1) * P].bitcast(FP8X4),
+                    lhsT_scale=scl[j][:, a * P : (a + 1) * P],
+                    rhs=w_codes[:, 2 * E : 3 * E].bitcast(FP8X4),
+                    rhs_scale=w_scales[:, 2 * E : 3 * E],
+                    start=True, stop=True,
+                )
+
+        def empty(j, bank, on_scalar):
+            pk0, pn = piece_of[2 * j]
+            js = 2 * j - pk0
+            if pk0 not in o_sb:
+                o_sb[pk0] = opool.tile([P, 6, pn, P], F32, tag="o_sb", name="o_sb%d" % pk0)
+            if bank < 2:
+                dst = o_sb[pk0][:, 0:4, js + bank, :]
+                src = banks[(j, bank)][:].rearrange("p (g d) -> p g d", d=P)
+            else:
+                dst = o_sb[pk0][:, 4:6, js : js + 2, :].rearrange("p g a d -> p a g d")
+                src = banks[(j, 2)][:].rearrange("p (a g d) -> p a g d", a=2, d=P)
+            if on_scalar:
+                nc.scalar.copy(out=dst, in_=src)
+            else:
+                nc.vector.tensor_copy(out=dst, in_=src)
+
+        def store(pk0):
+            pn = piece_of[pk0][1]
+            b, j0 = divmod(pk0, JB)
+            for i in range(3):
+                ov = outs[i][b].rearrange("h (p j) d -> p h j d", j=JB)
+                nc.sync.dma_start(
+                    out=ov[:, :, j0 : j0 + pn, :], in_=o_sb[pk0][:, 2 * i : 2 * i + 2, :, :]
+                )
+
+        statistics(2)
+        gain_columns()
+        for u in range(4):
+            w_transposes(u)
+        w_regroup(0)
+        release(0)
+        w_regroup(1)
+        statistics(2)
+        w_regroup(2)
+        release(1)
+        w_transposes(4)
+        w_regroup(3)
+        w_transposes(5)
+        statistics(HEAD_STATS - 4)
+        transposes(0)
+        w_regroup(4)
+        transposes(1)
+        norm(0)
+        w_regroup(5)
+        norm(1)
+        for i in range(3):
+            w_quantise(i)
+        quantise(0)
+        release(2)
+
+        waiting = []
+        stored = 0
+        for i in range(NP + 1):
+            if i + 1 < NP:
+                transposes(2 * i + 2)
+                transposes(2 * i + 3)
+            if i < NP:
+                project(i)
+            if i + 1 < NP:
+                norm(2 * i + 2)
+                norm(2 * i + 3)
+            for j, bank in waiting:
+                empty(j, bank, False)
+            waiting = []
+            if i + 1 < NP:
+                quantise(i + 1)
+            release(i + LEAD)
+            statistics(2)
+            if i < NP:
+                n_scalar = 3 if i >= S_ALL_FROM else S_BANKS[i % len(S_BANKS)]
+                for bank in range(3):
+                    if bank < n_scalar:
+                        empty(i, bank, True)
                     else:
-                        nc.scalar.copy(out=dst, in_=src)
-                nc.vector.tensor_copy(
-                    out=o_sb[:, 4:6, js : js + 2, :].rearrange("p g a d -> p a g d"),
-                    in_=o_v[:].rearrange("p (a g d) -> p a g d", a=2, d=P),
-                )
-                if js + 2 == pn:
-                    b, j0 = divmod(pk0, JB)
-                    for i in range(3):
-                        ov = outs[i][b].rearrange("h (p j) d -> p h j d", j=JB)
-                        nc.sync.dma_start(
-                            out=ov[:, :, j0 : j0 + pn, :], in_=o_sb[:, 2 * i : 2 * i + 2, :, :]
-                        )
-            first += gn
+                        waiting.append((i, bank))
+            done = i + 1 if (i < NP and not waiting) else i
+            while stored < min(done, NP):
+                pk0, pn = piece_of[2 * stored]
+                if 2 * stored + 2 == pk0 + pn:
+                    store(pk0)
+                stored += 1

@@ -21,16 +21,22 @@ PACK = 4
 JB = S // P
 CH = 4
 NT = B * JB
-NP = NT // 2
 NOUT = 3 * E
-STAT_GROUPS = [2, 2] + [4] * 15
+UNITS = [2, 2] + [4] * 14 + [2, 2]
 PIECES = [4] * 15 + [2, 2]
-HEAD_STATS = 12
-LEAD = 3
-S_BANKS = [1, 2]
-S_ALL_FROM = 26
+T_BANKS = 4
 
 FLOPS = 2 * B * S * D * NOUT
+
+
+def bank_plan(s, n, stats_done):
+    if s == len(UNITS) - 1:
+        return "SSv"
+    if n == 4:
+        return "SSSSSS" if stats_done else "SSVSVV"
+    if stats_done:
+        return "SSS"
+    return "SSV" if s % 2 == 1 else "SVV"
 
 
 def tile_transformerblock_pa_t_kernel(tc, x, g1, wq, wk, wv, out_0, out_1, out_2):
@@ -43,7 +49,7 @@ def tile_transformerblock_pa_t_kernel(tc, x, g1, wq, wk, wv, out_0, out_1, out_2
         stat = ctx.enter_context(tc.tile_pool(name="stat", bufs=1))
         work = ctx.enter_context(tc.tile_pool(name="work", bufs=3))
         opool = ctx.enter_context(tc.tile_pool(name="opool", bufs=6))
-        pt = ctx.enter_context(tc.psum_pool(name="pt", bufs=4))
+        pt = ctx.enter_context(tc.psum_pool(name="pt", bufs=T_BANKS))
         po = ctx.enter_context(tc.psum_pool(name="po", bufs=4))
         ctx.enter_context(tc.manual_schedule())
 
@@ -95,7 +101,7 @@ def tile_transformerblock_pa_t_kernel(tc, x, g1, wq, wk, wv, out_0, out_1, out_2
         w_ps = {}
 
         def w_transposes(u):
-            w_ps[u] = pt.tile([P, PACK, P], BF16, tag="t", name="w_ps%d" % u)
+            w_ps[u] = po.tile([P, PACK, P], BF16, tag="o", name="w_ps%d" % u)
             for t in range(PACK):
                 nc.tensor.transpose(
                     out=w_ps[u][:, t, :], in_=w_raw[u // 2][:, u % 2, t * P : (t + 1) * P],
@@ -114,12 +120,17 @@ def tile_transformerblock_pa_t_kernel(tc, x, g1, wq, wk, wv, out_0, out_1, out_2
                 in_=w_grp[:, i * E : (i + 1) * E, :].rearrange("p n t -> p (n t)"),
             )
 
-        group_of = []
+        unit_of = []
         k0 = 0
-        for gi, gn in enumerate(STAT_GROUPS):
-            for q in range(gn):
-                group_of.append((gi, k0, gn))
-            k0 += gn
+        for s, n in enumerate(UNITS):
+            for q in range(n):
+                unit_of.append((s, k0, n))
+            k0 += n
+        unit_first = []
+        k0 = 0
+        for n in UNITS:
+            unit_first.append(k0)
+            k0 += n
         piece_of = []
         k0 = 0
         for pn in PIECES:
@@ -137,72 +148,91 @@ def tile_transformerblock_pa_t_kernel(tc, x, g1, wq, wk, wv, out_0, out_1, out_2
         scl = {}
         banks = {}
         o_sb = {}
-        progress = {"stats": 0}
+        emptied = {}
+        at = {"stats": 0, "released": 0, "scaled": 0, "transposed": 0, "normed": 0, "stored": 0}
 
         def statistics(count):
             for q in range(count):
-                k = progress["stats"]
+                k = at["stats"]
                 if k >= NT:
                     return
-                gi, g0, gn = group_of[k]
-                if k == g0:
-                    ss[gi] = stat.tile([P, gn], F32, name="ss%d" % gi)
+                s, k_first, n = unit_of[k]
+                if k == k_first:
+                    ss[s] = stat.tile([P, n], F32, name="ss%d" % s)
                 junk = work.tile([P, D], BF16, tag="junk")
                 nc.scalar.activation(
-                    out=junk[:], in_=x_tile(k), func=ACT.Square, accum_out=ss[gi][:, k - g0 : k - g0 + 1]
+                    out=junk[:], in_=x_tile(k), func=ACT.Square,
+                    accum_out=ss[s][:, k - k_first : k - k_first + 1],
                 )
-                if k == g0 + gn - 1:
-                    var = stat.tile([P, gn], F32, name="var%d" % gi)
-                    rms[gi] = stat.tile([P, gn], F32, name="rms%d" % gi)
-                    nc.scalar.activation(out=var[:], in_=ss[gi][:], func=ACT.Copy, bias=EPS, scale=1.0 / D)
-                    nc.scalar.activation(out=rms[gi][:], in_=var[:], func=ACT.Sqrt)
-                progress["stats"] = k + 1
+                if k == k_first + n - 1:
+                    var = stat.tile([P, n], F32, name="var%d" % s)
+                    rms[s] = stat.tile([P, n], F32, name="rms%d" % s)
+                    nc.scalar.activation(out=var[:], in_=ss[s][:], func=ACT.Copy, bias=EPS, scale=1.0 / D)
+                    nc.scalar.activation(out=rms[s][:], in_=var[:], func=ACT.Sqrt)
+                at["stats"] = k + 1
 
-        def release(j):
-            if j >= NP:
+        def release():
+            s = at["released"]
+            if s >= len(UNITS):
                 return
-            gi, g0, gn = group_of[2 * j]
-            rstd[j] = stat.tile([P, 2], F32, name="rstd%d" % j)
-            nc.vector.reciprocal(out=rstd[j][:], in_=rms[gi][:, 2 * j - g0 : 2 * j - g0 + 2])
-            for a in range(2):
-                k = 2 * j + a
-                y[k] = work.tile([P, D], F32, tag="y", bufs=6, name="y%d" % k)
+            at["released"] = s + 1
+            k_first = unit_first[s]
+            n = UNITS[s]
+            while at["stats"] < k_first + n:
+                statistics(1)
+            rstd[s] = stat.tile([P, n], F32, name="rstd%d" % s)
+            nc.vector.reciprocal(out=rstd[s][:], in_=rms[s][:])
+            for q in range(n):
+                k = k_first + q
+                y[k] = work.tile([P, D], F32, tag="y", bufs=8, name="y%d" % k)
                 nc.gpsimd.tensor_scalar(
-                    out=y[k][:], in0=x_tile(k), scalar1=rstd[j][:, a : a + 1], scalar2=1.0,
+                    out=y[k][:], in0=x_tile(k), scalar1=rstd[s][:, q : q + 1], scalar2=1.0,
                     op0=ALU.mult, op1=ALU.mult,
                 )
+                at["scaled"] = k + 1
 
-        def transposes(k):
-            y_ps[k] = pt.tile([P, PACK, P], F32, tag="t", name="y_ps%d" % k)
-            for t in range(PACK):
-                nc.tensor.transpose(
-                    out=y_ps[k][:, t, :], in_=y[k][:, t * P : (t + 1) * P], identity=ident_f[:]
-                )
+        def transposes():
+            while (
+                at["transposed"] < NT
+                and at["transposed"] < at["scaled"]
+                and at["transposed"] - T_BANKS < at["normed"]
+            ):
+                k = at["transposed"]
+                y_ps[k] = pt.tile([P, PACK, P], F32, tag="t", name="y_ps%d" % k)
+                for t in range(PACK):
+                    nc.tensor.transpose(
+                        out=y_ps[k][:, t, :], in_=y[k][:, t * P : (t + 1) * P], identity=ident_f[:]
+                    )
+                at["transposed"] = k + 1
 
         def norm(k):
-            j = k // 2
-            if k % 2 == 0:
-                grp[j] = work.tile([P, 2, P, PACK], BF16, tag="grp", align_bytes=64, name="grp%d" % j)
+            s, k_first, n = unit_of[k]
+            if k == k_first:
+                grp[s] = work.tile([P, n, P, PACK], BF16, tag="grp", align_bytes=64, name="grp%d" % s)
             nc.vector.tensor_tensor(
-                out=grp[j][:, k % 2, :, :], in0=y_ps[k][:].rearrange("p t r -> p r t"), in1=gain_b,
+                out=grp[s][:, k - k_first, :, :], in0=y_ps[k][:].rearrange("p t r -> p r t"), in1=gain_b,
                 op=ALU.mult,
             )
+            at["normed"] = k + 1
 
-        def quantise(j):
-            codes[j] = work.tile([P, 2 * P], U32, tag="codes", align_bytes=64, name="codes%d" % j)
-            scl[j] = work.tile([P, 2 * P], U8, tag="scl", align_bytes=64, name="scl%d" % j)
+        def quantise(s):
+            n = UNITS[s]
+            codes[s] = work.tile([P, n * P], U32, tag="codes", align_bytes=64, name="codes%d" % s)
+            scl[s] = work.tile([P, n * P], U8, tag="scl", align_bytes=64, name="scl%d" % s)
             nc.vector.quantize_mx(
-                out=codes[j][:].bitcast(FP8X4), scales=scl[j][:],
-                in_=grp[j][:].rearrange("p a r t -> p (a r t)"),
+                out=codes[s][:].bitcast(FP8X4), scales=scl[s][:],
+                in_=grp[s][:].rearrange("p a r t -> p (a r t)"),
             )
 
         def project(j):
+            s, k_first, n = unit_of[2 * j]
+            c0 = (2 * j - k_first) * P
             for a in range(2):
                 banks[(j, a)] = po.tile([P, 2 * E], F32, tag="o", name="o%d_%d" % (j, a))
                 nc.tensor.matmul_mx(
                     out=banks[(j, a)][:],
-                    lhsT=codes[j][:, a * P : (a + 1) * P].bitcast(FP8X4),
-                    lhsT_scale=scl[j][:, a * P : (a + 1) * P],
+                    lhsT=codes[s][:, c0 + a * P : c0 + (a + 1) * P].bitcast(FP8X4),
+                    lhsT_scale=scl[s][:, c0 + a * P : c0 + (a + 1) * P],
                     rhs=w_codes[:, 0 : 2 * E].bitcast(FP8X4),
                     rhs_scale=w_scales[:, 0 : 2 * E],
                     start=True, stop=True,
@@ -211,11 +241,20 @@ def tile_transformerblock_pa_t_kernel(tc, x, g1, wq, wk, wv, out_0, out_1, out_2
             for a in range(2):
                 nc.tensor.matmul_mx(
                     out=banks[(j, 2)][:, a * E : (a + 1) * E],
-                    lhsT=codes[j][:, a * P : (a + 1) * P].bitcast(FP8X4),
-                    lhsT_scale=scl[j][:, a * P : (a + 1) * P],
+                    lhsT=codes[s][:, c0 + a * P : c0 + (a + 1) * P].bitcast(FP8X4),
+                    lhsT_scale=scl[s][:, c0 + a * P : c0 + (a + 1) * P],
                     rhs=w_codes[:, 2 * E : 3 * E].bitcast(FP8X4),
                     rhs_scale=w_scales[:, 2 * E : 3 * E],
                     start=True, stop=True,
+                )
+
+        def store(pk0):
+            pn = piece_of[pk0][1]
+            b, j0 = divmod(pk0, JB)
+            for i in range(3):
+                ov = outs[i][b].rearrange("h (p j) d -> p h j d", j=JB)
+                nc.sync.dma_start(
+                    out=ov[:, :, j0 : j0 + pn, :], in_=o_sb[pk0][:, 2 * i : 2 * i + 2, :, :]
                 )
 
         def empty(j, bank, on_scalar):
@@ -233,69 +272,67 @@ def tile_transformerblock_pa_t_kernel(tc, x, g1, wq, wk, wv, out_0, out_1, out_2
                 nc.scalar.copy(out=dst, in_=src)
             else:
                 nc.vector.tensor_copy(out=dst, in_=src)
-
-        def store(pk0):
-            pn = piece_of[pk0][1]
-            b, j0 = divmod(pk0, JB)
-            for i in range(3):
-                ov = outs[i][b].rearrange("h (p j) d -> p h j d", j=JB)
-                nc.sync.dma_start(
-                    out=ov[:, :, j0 : j0 + pn, :], in_=o_sb[pk0][:, 2 * i : 2 * i + 2, :, :]
-                )
+            emptied[j] = emptied.get(j, 0) + 1
+            while at["stored"] < NT // 2 and emptied.get(at["stored"], 0) == 3:
+                done = at["stored"]
+                first, count = piece_of[2 * done]
+                if 2 * done + 2 == first + count:
+                    store(first)
+                at["stored"] = done + 1
 
         statistics(2)
         gain_columns()
-        for u in range(4):
+        for u in range(6):
             w_transposes(u)
-        w_regroup(0)
-        release(0)
-        w_regroup(1)
+            if u == 3:
+                w_regroup(0)
+            if u == 4:
+                release()
+                w_regroup(1)
         statistics(2)
         w_regroup(2)
-        release(1)
-        w_transposes(4)
+        release()
         w_regroup(3)
-        w_transposes(5)
-        statistics(HEAD_STATS - 4)
-        transposes(0)
+        transposes()
         w_regroup(4)
-        transposes(1)
-        norm(0)
         w_regroup(5)
-        norm(1)
+        statistics(8)
         for i in range(3):
             w_quantise(i)
-        quantise(0)
-        release(2)
 
         waiting = []
-        stored = 0
-        for i in range(NP + 1):
-            if i + 1 < NP:
-                transposes(2 * i + 2)
-                transposes(2 * i + 3)
-            if i < NP:
-                project(i)
-            if i + 1 < NP:
-                norm(2 * i + 2)
-                norm(2 * i + 3)
+        for s, n in enumerate(UNITS):
+            k_first = unit_first[s]
+            for k in range(k_first, k_first + n):
+                norm(k)
+                transposes()
             for j, bank in waiting:
                 empty(j, bank, False)
             waiting = []
-            if i + 1 < NP:
-                quantise(i + 1)
-            release(i + LEAD)
-            statistics(2)
-            if i < NP:
-                n_scalar = 3 if i >= S_ALL_FROM else S_BANKS[i % len(S_BANKS)]
-                for bank in range(3):
-                    if bank < n_scalar:
-                        empty(i, bank, True)
-                    else:
-                        waiting.append((i, bank))
-            done = i + 1 if (i < NP and not waiting) else i
-            while stored < min(done, NP):
-                pk0, pn = piece_of[2 * stored]
-                if 2 * stored + 2 == pk0 + pn:
-                    store(pk0)
-                stored += 1
+            quantise(s)
+            release()
+            pairs = list(range(k_first // 2, (k_first + n) // 2))
+            for j in pairs:
+                project(j)
+            transposes()
+            plan = bank_plan(s, n, at["stats"] >= NT)
+            n_scalar = len([who for who in plan if who == "S"])
+            statistics((n + 1) // 2)
+            taken = 0
+            late_stats = n - (n + 1) // 2
+            for index, who in enumerate(plan):
+                j = pairs[index // 3]
+                bank = index % 3
+                if who == "S":
+                    empty(j, bank, True)
+                    taken += 1
+                    if taken == (n_scalar + 1) // 2:
+                        statistics(late_stats)
+                        late_stats = 0
+                elif who == "v":
+                    empty(j, bank, False)
+                else:
+                    waiting.append((j, bank))
+            statistics(late_stats)
+        for j, bank in waiting:
+            empty(j, bank, False)

@@ -66,7 +66,9 @@ def tile_transformerblock_pa_t_kernel(tc, x, g1, wq, wk, wv, out_0, out_1, out_2
         def x_tile(k):
             return xs[k // CH][:, k % CH, :]
 
-        load_x(0)
+        xv0 = x[0].rearrange("(p j) d -> p j d", j=JB)
+        nc.sync.dma_start(out=xs[0][:, 0:2, :], in_=xv0[:, 0:2, :])
+        nc.sync.dma_start(out=xs[0][:, 2:4, :], in_=xv0[:, 2:4, :])
         g_rows = const.tile([P, P], BF16)
         nc.vector.memset(g_rows[:], 0.0)
         nc.sync.dma_start(out=g_rows[0:PACK, :], in_=g1.rearrange("(t p) -> t p", p=P))
@@ -165,13 +167,11 @@ def tile_transformerblock_pa_t_kernel(tc, x, g1, wq, wk, wv, out_0, out_1, out_2
                     accum_out=ss[s][:, k - k_first : k - k_first + 1],
                 )
                 if k == k_first + n - 1:
-                    var = stat.tile([P, n], F32, name="var%d" % s)
                     rms[s] = stat.tile([P, n], F32, name="rms%d" % s)
-                    nc.scalar.activation(out=var[:], in_=ss[s][:], func=ACT.Copy, bias=EPS, scale=1.0 / D)
-                    nc.scalar.activation(out=rms[s][:], in_=var[:], func=ACT.Sqrt)
+                    nc.scalar.activation(out=rms[s][:], in_=ss[s][:], func=ACT.Sqrt, bias=EPS, scale=1.0 / D)
                 at["stats"] = k + 1
 
-        def release():
+        def reciprocal():
             s = at["released"]
             if s >= len(UNITS):
                 return
@@ -182,6 +182,13 @@ def tile_transformerblock_pa_t_kernel(tc, x, g1, wq, wk, wv, out_0, out_1, out_2
                 statistics(1)
             rstd[s] = stat.tile([P, n], F32, name="rstd%d" % s)
             nc.vector.reciprocal(out=rstd[s][:], in_=rms[s][:])
+
+        def scale():
+            s = at["released"] - 1
+            k_first = unit_first[s]
+            if at["scaled"] > k_first:
+                return
+            n = UNITS[s]
             for q in range(n):
                 k = k_first + q
                 y[k] = work.tile([P, D], F32, tag="y", bufs=8, name="y%d" % k)
@@ -287,11 +294,13 @@ def tile_transformerblock_pa_t_kernel(tc, x, g1, wq, wk, wv, out_0, out_1, out_2
             if u == 3:
                 w_regroup(0)
             if u == 4:
-                release()
+                reciprocal()
+                scale()
                 w_regroup(1)
         statistics(2)
         w_regroup(2)
-        release()
+        reciprocal()
+        scale()
         w_regroup(3)
         transposes()
         w_regroup(4)
@@ -309,8 +318,9 @@ def tile_transformerblock_pa_t_kernel(tc, x, g1, wq, wk, wv, out_0, out_1, out_2
             for j, bank in waiting:
                 empty(j, bank, False)
             waiting = []
+            reciprocal()
             quantise(s)
-            release()
+            scale()
             pairs = list(range(k_first // 2, (k_first + n) // 2))
             for j in pairs:
                 project(j)

@@ -193,8 +193,8 @@ def tile_transformerblock_pa_t_kernel(tc, x, g1, wq, wk, wv, out_0, out_1, out_2
                 k = k_first + q
                 y[k] = work.tile([P, D], F32, tag="y", bufs=8, name="y%d" % k)
                 nc.gpsimd.tensor_scalar(
-                    out=y[k][:], in0=x_tile(k), scalar1=rstd[s][:, q : q + 1], scalar2=1.0,
-                    op0=ALU.mult, op1=ALU.mult,
+                    out=y[k][:], in0=x_tile(k), scalar1=rstd[s][:, q : q + 1], scalar2=0.0,
+                    op0=ALU.mult, op1=ALU.add,
                 )
                 at["scaled"] = k + 1
 

@@ -69,9 +69,9 @@ def tile_transformerblock_pa_t_kernel(tc, x, g1, wq, wk, wv, out_0, out_1, out_2
         xv0 = x[0].rearrange("(p j) d -> p j d", j=JB)
         nc.sync.dma_start(out=xs[0][:, 0:2, :], in_=xv0[:, 0:2, :])
         nc.sync.dma_start(out=xs[0][:, 2:4, :], in_=xv0[:, 2:4, :])
-        g_rows = const.tile([P, P], BF16)
+        g_rows = const.tile([P, 2 * P], BF16)
         nc.vector.memset(g_rows[:], 0.0)
-        nc.sync.dma_start(out=g_rows[0:PACK, :], in_=g1.rearrange("(t p) -> t p", p=P))
+        nc.sync.dma_start(out=g_rows[0:2, :], in_=g1.rearrange("(u c) -> u c", u=2))
         w_raw = []
         for i in range(3):
             wr = const.tile([P, 2, D], BF16, name="w_raw%d" % i)
@@ -80,8 +80,6 @@ def tile_transformerblock_pa_t_kernel(tc, x, g1, wq, wk, wv, out_0, out_1, out_2
         for c in range(1, n_chunks):
             load_x(c)
 
-        ident_b = const.tile([P, P], BF16)
-        make_identity(nc, ident_b[:])
         ident_f = const.tile([P, P], F32)
         make_identity(nc, ident_f[:])
         one_t = const.tile([P, 1], F32)
@@ -96,23 +94,27 @@ def tile_transformerblock_pa_t_kernel(tc, x, g1, wq, wk, wv, out_0, out_1, out_2
         w_scales = const.tile([P, NOUT], U8, align_bytes=64)
 
         def gain_columns():
-            g_ps = pt.tile([P, P], BF16, tag="t")
-            nc.tensor.transpose(out=g_ps[:], in_=g_rows[:], identity=ident_b[:])
-            nc.vector.tensor_copy(out=gain[:], in_=g_ps[:, 0:PACK])
+            g_ps = pt.tile([P, P], F32, tag="t")
+            nc.tensor.transpose(out=g_ps[:], in_=g_rows[:].bitcast(F32), identity=ident_f[:])
+            nc.vector.tensor_copy(out=gain[:], in_=g_ps[:, 0:2].bitcast(BF16))
 
         w_ps = {}
 
-        def w_transposes(u):
-            w_ps[u] = po.tile([P, PACK, P], BF16, tag="o", name="w_ps%d" % u)
-            for t in range(PACK):
-                nc.tensor.transpose(
-                    out=w_ps[u][:, t, :], in_=w_raw[u // 2][:, u % 2, t * P : (t + 1) * P],
-                    identity=ident_b[:],
-                )
+        w_words = w_grp[:].rearrange("p n t -> p (n t)").bitcast(F32)
 
-        def w_regroup(u):
+        def w_transposes(i):
+            w_ps[i] = po.tile([P, 2, 2, P], F32, tag="o", name="w_ps%d" % i)
+            for a in range(2):
+                words = w_raw[i][:, a, :].bitcast(F32)
+                for u in range(2):
+                    nc.tensor.transpose(
+                        out=w_ps[i][:, a, u, :], in_=words[:, u * P : (u + 1) * P], identity=ident_f[:]
+                    )
+
+        def w_regroup(i):
             nc.vector.tensor_copy(
-                out=w_grp[:, u * P : (u + 1) * P, :], in_=w_ps[u][:].rearrange("p t n -> p n t")
+                out=w_words[:, i * 2 * E : (i + 1) * 2 * E].rearrange("p (a n u) -> p a n u", a=2, u=2),
+                in_=w_ps[i][:].rearrange("p a u n -> p a n u"),
             )
 
         def w_quantise(i):
@@ -193,7 +195,9 @@ def tile_transformerblock_pa_t_kernel(tc, x, g1, wq, wk, wv, out_0, out_1, out_2
                 k = k_first + q
                 y[k] = work.tile([P, D], F32, tag="y", bufs=8, name="y%d" % k)
                 nc.gpsimd.tensor_scalar(
-                    out=y[k][:], in0=x_tile(k), scalar1=rstd[s][:, q : q + 1], scalar2=0.0,
+                    out=y[k][:].rearrange("p (u e c) -> p u e c", u=2, e=2),
+                    in0=x_tile(k).rearrange("p (u c e) -> p u e c", u=2, e=2),
+                    scalar1=rstd[s][:, q : q + 1], scalar2=0.0,
                     op0=ALU.mult, op1=ALU.add,
                 )
                 at["scaled"] = k + 1
@@ -289,22 +293,17 @@ def tile_transformerblock_pa_t_kernel(tc, x, g1, wq, wk, wv, out_0, out_1, out_2
 
         statistics(2)
         gain_columns()
-        for u in range(6):
-            w_transposes(u)
-            if u == 3:
-                w_regroup(0)
-            if u == 4:
-                reciprocal()
-                scale()
-                w_regroup(1)
-        statistics(2)
-        w_regroup(2)
+        for i in range(3):
+            w_transposes(i)
         reciprocal()
         scale()
-        w_regroup(3)
+        w_regroup(0)
+        statistics(2)
+        w_regroup(1)
+        reciprocal()
+        scale()
         transposes()
-        w_regroup(4)
-        w_regroup(5)
+        w_regroup(2)
         statistics(8)
         for i in range(3):
             w_quantise(i)

@@ -326,9 +326,10 @@ def tile_transformerblock_pa_t_kernel(tc, x, g1, wq, wk, wv, out_0, out_1, out_2
             transposes()
             plan = bank_plan(s, n, at["stats"] >= NT)
             n_scalar = len([who for who in plan if who == "S"])
-            statistics((n + 1) // 2)
+            early_stats = 3 if n == 4 else 1
+            statistics(early_stats)
             taken = 0
-            late_stats = n - (n + 1) // 2
+            late_stats = n - early_stats
             for index, who in enumerate(plan):
                 j = pairs[index // 3]
                 bank = index % 3

@@ -235,61 +235,40 @@ def tile_transformerblock_pa_t_kernel(tc, x, g1, wq, wk, wv, out_0, out_1, out_2
                 in_=grp[s][:].rearrange("p a r t -> p (a r t)"),
             )
 
-        def project(j):
+        def project(j, i):
             s, k_first, n = unit_of[2 * j]
             c0 = (2 * j - k_first) * P
-            for a in range(2):
-                banks[(j, a)] = po.tile([P, 2 * E], F32, tag="o", name="o%d_%d" % (j, a))
-                nc.tensor.matmul_mx(
-                    out=banks[(j, a)][:],
-                    lhsT=codes[s][:, c0 + a * P : c0 + (a + 1) * P].bitcast(FP8X4),
-                    lhsT_scale=scl[s][:, c0 + a * P : c0 + (a + 1) * P],
-                    rhs=w_codes[:, 0 : 2 * E].bitcast(FP8X4),
-                    rhs_scale=w_scales[:, 0 : 2 * E],
-                    start=True, stop=True,
-                )
-            banks[(j, 2)] = po.tile([P, 2 * E], F32, tag="o", name="o%d_2" % j)
+            banks[(j, i)] = po.tile([P, 2 * E], F32, tag="o", name="o%d_%d" % (j, i))
             for a in range(2):
                 nc.tensor.matmul_mx(
-                    out=banks[(j, 2)][:, a * E : (a + 1) * E],
+                    out=banks[(j, i)][:, a * E : (a + 1) * E],
                     lhsT=codes[s][:, c0 + a * P : c0 + (a + 1) * P].bitcast(FP8X4),
                     lhsT_scale=scl[s][:, c0 + a * P : c0 + (a + 1) * P],
-                    rhs=w_codes[:, 2 * E : 3 * E].bitcast(FP8X4),
-                    rhs_scale=w_scales[:, 2 * E : 3 * E],
+                    rhs=w_codes[:, i * E : (i + 1) * E].bitcast(FP8X4),
+                    rhs_scale=w_scales[:, i * E : (i + 1) * E],
                     start=True, stop=True,
                 )
 
-        def store(pk0):
+        def store(pk0, i):
             pn = piece_of[pk0][1]
             b, j0 = divmod(pk0, JB)
-            for i in range(3):
-                ov = outs[i][b].rearrange("h (p j) d -> p h j d", j=JB)
-                nc.sync.dma_start(
-                    out=ov[:, :, j0 : j0 + pn, :], in_=o_sb[pk0][:, 2 * i : 2 * i + 2, :, :]
-                )
+            ov = outs[i][b].rearrange("h (p j) d -> p h j d", j=JB)
+            nc.sync.dma_start(out=ov[:, :, j0 : j0 + pn, :], in_=o_sb[pk0][:, 2 * i : 2 * i + 2, :, :])
 
         def empty(j, bank, on_scalar):
             pk0, pn = piece_of[2 * j]
             js = 2 * j - pk0
             if pk0 not in o_sb:
                 o_sb[pk0] = opool.tile([P, 6, pn, P], F32, tag="o_sb", name="o_sb%d" % pk0)
-            if bank < 2:
-                dst = o_sb[pk0][:, 0:4, js + bank, :]
-                src = banks[(j, bank)][:].rearrange("p (g d) -> p g d", d=P)
-            else:
-                dst = o_sb[pk0][:, 4:6, js : js + 2, :].rearrange("p g a d -> p a g d")
-                src = banks[(j, 2)][:].rearrange("p (a g d) -> p a g d", a=2, d=P)
+            dst = o_sb[pk0][:, 2 * bank : 2 * bank + 2, js : js + 2, :].rearrange("p g a d -> p a g d")
+            src = banks[(j, bank)][:].rearrange("p (a g d) -> p a g d", a=2, d=P)
             if on_scalar:
                 nc.scalar.copy(out=dst, in_=src)
             else:
                 nc.vector.tensor_copy(out=dst, in_=src)
-            emptied[j] = emptied.get(j, 0) + 1
-            while at["stored"] < NT // 2 and emptied.get(at["stored"], 0) == 3:
-                done = at["stored"]
-                first, count = piece_of[2 * done]
-                if 2 * done + 2 == first + count:
-                    store(first)
-                at["stored"] = done + 1
+            emptied[(pk0, bank)] = emptied.get((pk0, bank), 0) + 2
+            if emptied[(pk0, bank)] == pn:
+                store(pk0, bank)
 
         statistics(2)
         gain_columns()
@@ -321,8 +300,9 @@ def tile_transformerblock_pa_t_kernel(tc, x, g1, wq, wk, wv, out_0, out_1, out_2
             quantise(s)
             scale()
             pairs = list(range(k_first // 2, (k_first + n) // 2))
-            for j in pairs:
-                project(j)
+            for i in range(3):
+                for j in pairs:
+                    project(j, i)
             transposes()
             plan = bank_plan(s, n, at["stats"] >= NT)
             n_scalar = len([who for who in plan if who == "S"])
@@ -331,8 +311,8 @@ def tile_transformerblock_pa_t_kernel(tc, x, g1, wq, wk, wv, out_0, out_1, out_2
             taken = 0
             late_stats = n - early_stats
             for index, who in enumerate(plan):
-                j = pairs[index // 3]
-                bank = index % 3
+                j = pairs[index % len(pairs)]
+                bank = index // len(pairs)
                 if who == "S":
                     empty(j, bank, True)
                     taken += 1

@@ -22,8 +22,8 @@ JB = S // P
 CH = 4
 NT = B * JB
 NOUT = 3 * E
-UNITS = [2, 2] + [4] * 14 + [2, 2]
-PIECES = [4] * 15 + [2, 2]
+UNITS = [2, 2] + [4] * 15
+PIECES = [4] * 16
 T_BANKS = 4
 
 FLOPS = 2 * B * S * D * NOUT
@@ -31,7 +31,7 @@ FLOPS = 2 * B * S * D * NOUT
 
 def bank_plan(s, n, stats_done):
     if s == len(UNITS) - 1:
-        return "SSv"
+        return "SvSvSv"
     if n == 4:
         return "SSSSSS" if stats_done else "SSVSVV"
     if stats_done:

from contextlib import ExitStack

import concourse.mybir as mybir
from concourse.masks import make_identity

F32 = mybir.dt.float32
BF16 = mybir.dt.bfloat16
U32 = mybir.dt.uint32
U8 = mybir.dt.uint8
FP8X4 = mybir.dt.float8_e4m3fn_x4
ACT = mybir.ActivationFunctionType
ALU = mybir.AluOpType

P = 128
B = 4
S = 2048
D = 512
E = 256
EPS = 1e-5
PACK = 4
JB = S // P
CH = 4
NT = B * JB
NOUT = 3 * E
UNITS = [2, 2] + [4] * 15
PIECES = [4] * 16
T_BANKS = 4

FLOPS = 2 * B * S * D * NOUT


def bank_plan(s, n, stats_done):
    if s == len(UNITS) - 1:
        return "SvSvSv"
    if n == 4:
        return "SSSSSS" if stats_done else "SSVSVV"
    if stats_done:
        return "SSS"
    return "SSV" if s % 2 == 1 else "SVV"


def tile_transformerblock_pa_t_kernel(tc, x, g1, wq, wk, wv, out_0, out_1, out_2):
    nc = tc.nc
    outs = [out_0, out_1, out_2]
    ws = [wq, wk, wv]
    with ExitStack() as ctx:
        const = ctx.enter_context(tc.tile_pool(name="const", bufs=1))
        xpool = ctx.enter_context(tc.tile_pool(name="xpool", bufs=1))
        stat = ctx.enter_context(tc.tile_pool(name="stat", bufs=1))
        work = ctx.enter_context(tc.tile_pool(name="work", bufs=3))
        opool = ctx.enter_context(tc.tile_pool(name="opool", bufs=6))
        pt = ctx.enter_context(tc.psum_pool(name="pt", bufs=T_BANKS))
        po = ctx.enter_context(tc.psum_pool(name="po", bufs=4))
        ctx.enter_context(tc.manual_schedule())

        n_chunks = NT // CH
        xs = []
        for c in range(n_chunks):
            xs.append(xpool.tile([P, CH, D], BF16, name="x%d" % c))

        def load_x(c):
            b, j0 = divmod(c * CH, JB)
            xv = x[b].rearrange("(p j) d -> p j d", j=JB)
            nc.sync.dma_start(out=xs[c][:], in_=xv[:, j0 : j0 + CH, :])

        def x_tile(k):
            return xs[k // CH][:, k % CH, :]

        xv0 = x[0].rearrange("(p j) d -> p j d", j=JB)
        nc.sync.dma_start(out=xs[0][:, 0:2, :], in_=xv0[:, 0:2, :])
        nc.sync.dma_start(out=xs[0][:, 2:4, :], in_=xv0[:, 2:4, :])
        g_rows = const.tile([P, 2 * P], BF16)
        nc.vector.memset(g_rows[:], 0.0)
        nc.sync.dma_start(out=g_rows[0:2, :], in_=g1.rearrange("(u c) -> u c", u=2))
        w_raw = []
        for i in range(3):
            wr = const.tile([P, 2, D], BF16, name="w_raw%d" % i)
            nc.sync.dma_start(out=wr[:], in_=ws[i].rearrange("(a p) k -> p a k", p=P))
            w_raw.append(wr)
        for c in range(1, n_chunks):
            load_x(c)

        ident_f = const.tile([P, P], F32)
        make_identity(nc, ident_f[:])
        one_t = const.tile([P, 1], F32)
        nc.vector.memset(one_t[:], 1.0)
        warm = const.tile([P, 1], F32)
        nc.scalar.activation(out=warm[:], in_=one_t[:], func=ACT.Sqrt)

        gain = const.tile([P, PACK], F32)
        gain_b = gain[:].unsqueeze(1).to_broadcast([P, P, PACK])
        w_grp = const.tile([P, NOUT, PACK], BF16, align_bytes=64)
        w_codes = const.tile([P, NOUT], U32, align_bytes=64)
        w_scales = const.tile([P, NOUT], U8, align_bytes=64)

        def gain_columns():
            g_ps = pt.tile([P, P], F32, tag="t")
            nc.tensor.transpose(out=g_ps[:], in_=g_rows[:].bitcast(F32), identity=ident_f[:])
            nc.vector.tensor_copy(out=gain[:], in_=g_ps[:, 0:2].bitcast(BF16))

        w_ps = {}

        w_words = w_grp[:].rearrange("p n t -> p (n t)").bitcast(F32)

        def w_transposes(i):
            w_ps[i] = po.tile([P, 2, 2, P], F32, tag="o", name="w_ps%d" % i)
            for a in range(2):
                words = w_raw[i][:, a, :].bitcast(F32)
                for u in range(2):
                    nc.tensor.transpose(
                        out=w_ps[i][:, a, u, :], in_=words[:, u * P : (u + 1) * P], identity=ident_f[:]
                    )

        def w_regroup(i):
            nc.vector.tensor_copy(
                out=w_words[:, i * 2 * E : (i + 1) * 2 * E].rearrange("p (a n u) -> p a n u", a=2, u=2),
                in_=w_ps[i][:].rearrange("p a u n -> p a n u"),
            )

        def w_quantise(i):
            nc.vector.quantize_mx(
                out=w_codes[:, i * E : (i + 1) * E].bitcast(FP8X4),
                scales=w_scales[:, i * E : (i + 1) * E],
                in_=w_grp[:, i * E : (i + 1) * E, :].rearrange("p n t -> p (n t)"),
            )

        unit_of = []
        k0 = 0
        for s, n in enumerate(UNITS):
            for q in range(n):
                unit_of.append((s, k0, n))
            k0 += n
        unit_first = []
        k0 = 0
        for n in UNITS:
            unit_first.append(k0)
            k0 += n
        piece_of = []
        k0 = 0
        for pn in PIECES:
            for q in range(pn):
                piece_of.append((k0, pn))
            k0 += pn

        ss = {}
        rms = {}
        rstd = {}
        y = {}
        y_ps = {}
        grp = {}
        codes = {}
        scl = {}
        banks = {}
        o_sb = {}
        emptied = {}
        at = {"stats": 0, "released": 0, "scaled": 0, "transposed": 0, "normed": 0, "stored": 0}

        def statistics(count):
            for q in range(count):
                k = at["stats"]
                if k >= NT:
                    return
                s, k_first, n = unit_of[k]
                if k == k_first:
                    ss[s] = stat.tile([P, n], F32, name="ss%d" % s)
                junk = work.tile([P, D], BF16, tag="junk")
                nc.scalar.activation(
                    out=junk[:], in_=x_tile(k), func=ACT.Square,
                    accum_out=ss[s][:, k - k_first : k - k_first + 1],
                )
                if k == k_first + n - 1:
                    rms[s] = stat.tile([P, n], F32, name="rms%d" % s)
                    nc.scalar.activation(out=rms[s][:], in_=ss[s][:], func=ACT.Sqrt, bias=EPS, scale=1.0 / D)
                at["stats"] = k + 1

        def reciprocal():
            s = at["released"]
            if s >= len(UNITS):
                return
            at["released"] = s + 1
            k_first = unit_first[s]
            n = UNITS[s]
            while at["stats"] < k_first + n:
                statistics(1)
            rstd[s] = stat.tile([P, n], F32, name="rstd%d" % s)
            nc.vector.reciprocal(out=rstd[s][:], in_=rms[s][:])

        def scale():
            s = at["released"] - 1
            k_first = unit_first[s]
            if at["scaled"] > k_first:
                return
            n = UNITS[s]
            for q in range(n):
                k = k_first + q
                y[k] = work.tile([P, D], F32, tag="y", bufs=8, name="y%d" % k)
                nc.gpsimd.tensor_scalar(
                    out=y[k][:].rearrange("p (u e c) -> p u e c", u=2, e=2),
                    in0=x_tile(k).rearrange("p (u c e) -> p u e c", u=2, e=2),
                    scalar1=rstd[s][:, q : q + 1], scalar2=0.0,
                    op0=ALU.mult, op1=ALU.add,
                )
                at["scaled"] = k + 1

        def transposes():
            while (
                at["transposed"] < NT
                and at["transposed"] < at["scaled"]
                and at["transposed"] - T_BANKS < at["normed"]
            ):
                k = at["transposed"]
                y_ps[k] = pt.tile([P, PACK, P], F32, tag="t", name="y_ps%d" % k)
                for t in range(PACK):
                    nc.tensor.transpose(
                        out=y_ps[k][:, t, :], in_=y[k][:, t * P : (t + 1) * P], identity=ident_f[:]
                    )
                at["transposed"] = k + 1

        def norm(k):
            s, k_first, n = unit_of[k]
            if k == k_first:
                grp[s] = work.tile([P, n, P, PACK], BF16, tag="grp", align_bytes=64, name="grp%d" % s)
            nc.vector.tensor_tensor(
                out=grp[s][:, k - k_first, :, :], in0=y_ps[k][:].rearrange("p t r -> p r t"), in1=gain_b,
                op=ALU.mult,
            )
            at["normed"] = k + 1

        def quantise(s):
            n = UNITS[s]
            codes[s] = work.tile([P, n * P], U32, tag="codes", align_bytes=64, name="codes%d" % s)
            scl[s] = work.tile([P, n * P], U8, tag="scl", align_bytes=64, name="scl%d" % s)
            nc.vector.quantize_mx(
                out=codes[s][:].bitcast(FP8X4), scales=scl[s][:],
                in_=grp[s][:].rearrange("p a r t -> p (a r t)"),
            )

        def project(j, i):
            s, k_first, n = unit_of[2 * j]
            c0 = (2 * j - k_first) * P
            banks[(j, i)] = po.tile([P, 2 * E], F32, tag="o", name="o%d_%d" % (j, i))
            for a in range(2):
                nc.tensor.matmul_mx(
                    out=banks[(j, i)][:, a * E : (a + 1) * E],
                    lhsT=codes[s][:, c0 + a * P : c0 + (a + 1) * P].bitcast(FP8X4),
                    lhsT_scale=scl[s][:, c0 + a * P : c0 + (a + 1) * P],
                    rhs=w_codes[:, i * E : (i + 1) * E].bitcast(FP8X4),
                    rhs_scale=w_scales[:, i * E : (i + 1) * E],
                    start=True, stop=True,
                )

        def store(pk0, i):
            pn = piece_of[pk0][1]
            b, j0 = divmod(pk0, JB)
            ov = outs[i][b].rearrange("h (p j) d -> p h j d", j=JB)
            nc.sync.dma_start(out=ov[:, :, j0 : j0 + pn, :], in_=o_sb[pk0][:, 2 * i : 2 * i + 2, :, :])

        def empty(j, bank, on_scalar):
            pk0, pn = piece_of[2 * j]
            js = 2 * j - pk0
            if pk0 not in o_sb:
                o_sb[pk0] = opool.tile([P, 6, pn, P], F32, tag="o_sb", name="o_sb%d" % pk0)
            dst = o_sb[pk0][:, 2 * bank : 2 * bank + 2, js : js + 2, :].rearrange("p g a d -> p a g d")
            src = banks[(j, bank)][:].rearrange("p (a g d) -> p a g d", a=2, d=P)
            if on_scalar:
                nc.scalar.copy(out=dst, in_=src)
            else:
                nc.vector.tensor_copy(out=dst, in_=src)
            emptied[(pk0, bank)] = emptied.get((pk0, bank), 0) + 2
            if emptied[(pk0, bank)] == pn:
                store(pk0, bank)

        statistics(2)
        gain_columns()
        for i in range(3):
            w_transposes(i)
        reciprocal()
        scale()
        w_regroup(0)
        statistics(2)
        w_regroup(1)
        reciprocal()
        scale()
        transposes()
        w_regroup(2)
        statistics(8)
        for i in range(3):
            w_quantise(i)

        waiting = []
        for s, n in enumerate(UNITS):
            k_first = unit_first[s]
            for k in range(k_first, k_first + n):
                norm(k)
                transposes()
            for j, bank in waiting:
                empty(j, bank, False)
            waiting = []
            reciprocal()
            quantise(s)
            scale()
            pairs = list(range(k_first // 2, (k_first + n) // 2))
            for i in range(3):
                for j in pairs:
                    project(j, i)
            transposes()
            plan = bank_plan(s, n, at["stats"] >= NT)
            n_scalar = len([who for who in plan if who == "S"])
            early_stats = 3 if n == 4 else 1
            statistics(early_stats)
            taken = 0
            late_stats = n - early_stats
            for index, who in enumerate(plan):
                j = pairs[index % len(pairs)]
                bank = index // len(pairs)
                if who == "S":
                    empty(j, bank, True)
                    taken += 1
                    if taken == (n_scalar + 1) // 2:
                        statistics(late_stats)
                        late_stats = 0
                elif who == "v":
                    empty(j, bank, False)
                else:
                    waiting.append((j, bank))
            statistics(late_stats)
        for j, bank in waiting:
            empty(j, bank, False)
